import numpy as np
import ml_dtypes


def mxq(x, axis, fmt="e4m3"):
    dtype, down = {"e4m3": (ml_dtypes.float8_e4m3fn, 7), "e5m2": (ml_dtypes.float8_e5m2, 14)}[fmt]
    v = np.moveaxis(np.asarray(x, np.float32).astype(ml_dtypes.bfloat16).astype(np.float64), axis, -1)
    blocks = v.reshape(v.shape[:-1] + (-1, 32))
    amax = np.abs(blocks).max(-1, keepdims=True)
    byte = np.maximum(np.where(amax > 0, np.frexp(amax)[1] - 1 + 127, 0) - down, 1)
    scale = np.exp2(byte - 127.0)
    codes = (blocks / scale).astype(np.float32).astype(dtype).astype(np.float64)
    return np.moveaxis((codes * scale).reshape(v.shape), -1, axis)


WIDE = False


def mx_kscale(k):
    if not WIDE:
        return np.ones(k)
    levels = np.array([10, -10, 5, -5, 0])
    a = np.random.permutation(np.resize(levels, k // 512 * 4)).reshape(k // 512, 4)
    idx = np.arange(k)
    return np.exp2(a[idx // 512, idx % 128 // 32])


BF16 = ml_dtypes.bfloat16


def bf(x):
    return np.asarray(x, np.float32).astype(BF16)


def f64(x):
    return np.asarray(x).astype(np.float64)


E2M1 = np.array([0.0, 0.5, 1.0, 1.5, 2.0, 3.0, 4.0, 6.0, -0.0, -0.5, -1.0, -1.5, -2.0, -3.0, -4.0, -6.0])


def pack_weight(w, fmt):
    k, n = w.shape
    w = f64(bf(w)).reshape(k // 32, 32, n)
    amax = np.abs(w).max(1)
    if fmt == "e4m3":
        byte = np.frexp(amax)[1] - 1 + 127 - 7
    else:
        mant, ex = np.frexp(amax / 6.0)
        byte = np.where(mant > 0.5, ex, ex - 1) + 127
    byte = np.clip(np.where(amax > 0, byte, 1), 1, 254)
    scaled = (w * np.exp2(127.0 - byte)[:, None, :]).reshape(k, n).astype(np.float32)
    by_word = np.ascontiguousarray(scaled.reshape(k // 512, 128, 4, n).transpose(0, 1, 3, 2))
    if fmt == "e4m3":
        words = by_word.astype(ml_dtypes.float8_e4m3fn).view(np.uint8)
    else:
        c = by_word.astype(ml_dtypes.float4_e2m1fn).view(np.uint8) & 0xF
        words = c[..., 0::2] | (c[..., 1::2] << 4)
    return np.ascontiguousarray(words), np.ascontiguousarray(byte.astype(np.uint8).reshape(k // 512, 16, n))


def unpack_weight(words, scales, fmt):
    g, p, n, _ = words.shape
    if fmt == "e4m3":
        vals = np.ascontiguousarray(words).view(ml_dtypes.float8_e4m3fn).astype(np.float64)
    else:
        nib = np.empty((g, p, n, 4), np.uint8)
        nib[..., 0::2] = words & 0xF
        nib[..., 1::2] = words >> 4
        vals = E2M1[nib]
    vals = vals * np.repeat(np.exp2(scales.astype(np.float64) - 127.0), 8, axis=1)[..., None]
    return vals.transpose(0, 1, 3, 2).reshape(g * 512, n)


B, P0, P1, P2, K0, K1, K2 = 128, 512, 1152, 896, 8192, 8192, 8192
PT = P0 + P1 + P2
KT = K0 + K1 + K2
CLIP1 = 1.0
FMT = "e4m3"


def clip_rows(mat, clip):
    norms = np.sqrt(np.sum(mat * mat, axis=1, keepdims=True))
    scale = np.minimum(clip / norms, 1.0)
    return mat * scale


def setup_inputs():
    t0, t1, t2 = mx_kscale(K0), mx_kscale(K1), mx_kscale(K2)
    r = np.exp2(np.random.uniform(-2.0, 2.0, (B, 1))) / (KT * PT) ** 0.25
    target_grad = bf(np.random.standard_normal((B, PT)) * r)
    embedding = bf(np.random.standard_normal((B, KT)) * r * np.concatenate([t0, t1, t2]))
    words0, scales0 = pack_weight(np.ascontiguousarray((np.random.standard_normal((P0, K0)) / np.sqrt(P0) / t0[None, :]).T), FMT)
    words1, scales1 = pack_weight(np.ascontiguousarray((np.random.standard_normal((P1, K1)) / np.sqrt(P1) / t1[None, :]).T), FMT)
    words2, scales2 = pack_weight(np.ascontiguousarray((np.random.standard_normal((P2, K2)) / np.sqrt(P2) / t2[None, :]).T), FMT)
    return {"target_grad": target_grad,
            "embedding": embedding,
            "bases0_words": words0, "bases0_scales": scales0,
            "bases1_words": words1, "bases1_scales": scales1,
            "bases2_words": words2, "bases2_scales": scales2}


def reference(target_grad, embedding, bases0_words, bases0_scales, bases1_words, bases1_scales, bases2_words, bases2_scales):
    g = f64(target_grad)
    e = f64(embedding)
    approx_parts = []
    offset = 0
    for bt in (unpack_weight(bases0_words, bases0_scales, FMT),
               unpack_weight(bases1_words, bases1_scales, FMT),
               unpack_weight(bases2_words, bases2_scales, FMT)):
        num_k = bt.shape[0]
        approx_parts.append(mxq(e[:, offset:offset + num_k], 1, "e4m3") @ bt)
        offset += num_k
    no_reduction_approx = np.concatenate(approx_parts, axis=1)
    residual = g - no_reduction_approx
    return np.sum(clip_rows(residual, CLIP1), axis=0) / B

@@ -1,0 +1,218 @@
+from contextlib import ExitStack
+
+import concourse.mybir as mybir
+from concourse.masks import make_identity
+
+F32 = mybir.dt.float32
+BF16 = mybir.dt.bfloat16
+I32 = mybir.dt.int32
+U32 = mybir.dt.uint32
+U8 = mybir.dt.uint8
+FP8X4 = mybir.dt.float8_e4m3fn_x4
+ACT = mybir.ActivationFunctionType
+ALU = mybir.AluOpType
+
+P = 128
+BATCH = 128
+PACK = 4
+K_PASS = P * PACK
+PASSES = 16
+BASE_COLS = (512, 1152, 896)
+FIRST_COL = (0, 512, 1664)
+ALL_COLS = 2560
+CLIP = 1.0
+BANK = 512
+
+BASE_ORDER = (1, 2, 0)
+
+UNIT = 4
+X_LOAD = 8
+OFFSETS = 4
+W_BYTES = 9216
+W_BUFS = 10
+PIECE = 256
+
+FLOPS = 2 * BATCH * PASSES * K_PASS * ALL_COLS
+
+
+def cut_columns(total):
+    groups = []
+    start = 0
+    for width in (512, 256, 128):
+        while total - start >= width:
+            groups.append((start, width))
+            start += width
+    return groups
+
+
+def cut_passes(per_load, taper):
+    sizes = [per_load] * (PASSES // per_load)
+    if taper:
+        last = sizes.pop()
+        while last > 1:
+            last //= 2
+            sizes.append(last)
+        sizes.append(last)
+    return sizes
+
+
+def tile_gep_pb_k_kernel(
+    tc,
+    target_grad,
+    embedding,
+    bases0_words,
+    bases0_scales,
+    bases1_words,
+    bases1_scales,
+    bases2_words,
+    bases2_scales,
+    out,
+):
+    nc = tc.nc
+    words = (bases0_words, bases1_words, bases2_words)
+    scales = (bases0_scales, bases1_scales, bases2_scales)
+
+    with ExitStack() as ctx:
+        ctx.enter_context(tc.manual_schedule())
+        keep = ctx.enter_context(tc.tile_pool(name="keep", bufs=1))
+        x_pool = ctx.enter_context(tc.tile_pool(name="x_pool", bufs=3 * PASSES // X_LOAD))
+        stage = ctx.enter_context(tc.tile_pool(name="stage", bufs=3))
+        w_pool = ctx.enter_context(tc.tile_pool(name="w_pool", bufs=W_BUFS))
+        psum_work = ctx.enter_context(tc.psum_pool(name="psum_work", bufs=5))
+        psum_acc = ctx.enter_context(tc.psum_pool(name="psum_acc", bufs=1))
+
+        planes = {}
+        for i in BASE_ORDER:
+            planes[i] = keep.tile(
+                [P, PASSES // OFFSETS, BASE_COLS[i]], U8, name="planes%d" % i, align_bytes=64
+            )
+            nc.vector.memset(planes[i][:].bitcast(I32), 0)
+        one = keep.tile([P, 1], F32)
+        nc.vector.memset(one[:], 1.0)
+        warm = keep.tile([P, 1], F32)
+        nc.scalar.activation(out=warm[:], in_=one[:], func=ACT.Abs_reciprocal_sqrt)
+        ident = keep.tile([P, P], F32)
+        make_identity(nc, ident[:])
+
+        x_codes = keep.tile([P, 3 * PASSES, BATCH], U32, align_bytes=64)
+        x_scales = keep.tile([P, 3 * PASSES, BATCH], U8, align_bytes=64)
+        grad = keep.tile([P, ALL_COLS], BF16)
+        resid = keep.tile([P, ALL_COLS], F32)
+        squares = keep.tile([P, ALL_COLS], F32)
+        mean_row = keep.tile([P, ALL_COLS], F32)
+        sum_sq = keep.tile([P, ALL_COLS // P], F32)
+
+        x_words = {}
+        for i in BASE_ORDER:
+            for load in range(PASSES // X_LOAD):
+                first_pass = PASSES * i + X_LOAD * load
+                x_sb = x_pool.tile([P, X_LOAD * K_PASS], BF16)
+                nc.sync.dma_start(
+                    out=x_sb[:],
+                    in_=embedding[:, K_PASS * first_pass : K_PASS * (first_pass + X_LOAD)],
+                )
+                for g in range(X_LOAD):
+                    x_words[first_pass + g] = x_sb[:, K_PASS * g : K_PASS * (g + 1)].bitcast(F32)
+        nc.sync.dma_start(out=grad[:], in_=target_grad)
+        for i in BASE_ORDER:
+            for G in range(PASSES // OFFSETS):
+                for Q in range(4):
+                    nc.sync.dma_start(
+                        out=planes[i][32 * Q : 32 * Q + 16, G, :].bitcast(I32),
+                        in_=scales[i][OFFSETS * G : OFFSETS * (G + 1), 4 * Q : 4 * Q + 4, :].bitcast(I32),
+                    )
+
+        def regroup(unit):
+            grouped = stage.tile([P, UNIT, BATCH, PACK], BF16, align_bytes=64)
+            grouped_words = grouped[:].bitcast(F32)
+            for half in range(2):
+                xt = psum_work.tile([P, UNIT // 2, 2, BATCH], F32, name="xt", tag="work")
+                for j in range(UNIT // 2):
+                    x_pass = UNIT * unit + (UNIT // 2) * half + j
+                    for u in range(2):
+                        nc.tensor.transpose(xt[:, j, u, :], x_words[x_pass][:, u : K_PASS // 2 : 2], ident[:])
+                dst = grouped_words[:, (UNIT // 2) * half : (UNIT // 2) * (half + 1), :, :]
+                src = xt[:].rearrange("p j u b -> p j b u")
+                if half == 0:
+                    nc.scalar.copy(out=dst, in_=src)
+                else:
+                    nc.vector.tensor_copy(out=dst, in_=src)
+            return grouped
+
+        def quantise(unit, grouped):
+            passes = slice(UNIT * unit, UNIT * (unit + 1))
+            nc.vector.quantize_mx(
+                out=x_codes[:, passes, :].rearrange("p g b -> p (g b)").bitcast(FP8X4),
+                scales=x_scales[:, passes, :].rearrange("p g b -> p (g b)"),
+                in_=grouped[:].rearrange("p g b t -> p (g b t)"),
+            )
+
+        units = [PASSES // UNIT * i + n for i in BASE_ORDER for n in range(PASSES // UNIT)]
+        waiting = None
+        for unit in units:
+            grouped = regroup(unit)
+            if waiting is not None:
+                quantise(waiting[0], waiting[1])
+            waiting = (unit, grouped)
+        quantise(waiting[0], waiting[1])
+
+        pieces_done = 0
+        for i in BASE_ORDER:
+            row_bytes = PACK * BASE_COLS[i]
+            groups = cut_columns(BASE_COLS[i])
+            acc = [psum_acc.tile([P, BANK], F32, name="acc%d" % n) for n in range(len(groups))]
+            g = 0
+            for n_passes in cut_passes(W_BYTES // row_bytes, taper=(i == BASE_ORDER[-1])):
+                w = w_pool.tile([P, W_BYTES], U8, align_bytes=64)
+                nc.sync.dma_start(
+                    out=w[:, : n_passes * row_bytes].bitcast(I32).rearrange("p (g c) -> p g c", g=n_passes),
+                    in_=words[i][g : g + n_passes].rearrange("g p n t -> p g (n t)").bitcast(I32),
+                )
+                for local in range(n_passes):
+                    for n, (start, width) in enumerate(groups):
+                        first_byte = local * row_bytes + PACK * start
+                        nc.tensor.matmul_mx(
+                            out=acc[n][:, :width],
+                            lhsT=x_codes[:, PASSES * i + g, :].bitcast(FP8X4),
+                            lhsT_scale=x_scales[:, PASSES * i + g, :],
+                            rhs=w[:, first_byte : first_byte + PACK * width].bitcast(FP8X4),
+                            rhs_scale=planes[i][4 * (g % OFFSETS) : P, g // OFFSETS, start : start + width],
+                            start=(g == 0),
+                            stop=(g == PASSES - 1),
+                        )
+                    g += 1
+            for n, (start, width) in enumerate(groups):
+                for first in range(0, width, PIECE):
+                    size = min(PIECE, width - first)
+                    cols = slice(FIRST_COL[i] + start + first, FIRST_COL[i] + start + first + size)
+                    nc.vector.tensor_tensor(
+                        out=resid[:, cols], in0=grad[:, cols], in1=acc[n][:, first : first + size], op=ALU.subtract
+                    )
+                    nc.scalar.activation(
+                        out=squares[:, cols],
+                        in_=resid[:, cols],
+                        func=ACT.Square,
+                        accum_out=sum_sq[:, pieces_done : pieces_done + 1],
+                    )
+                    pieces_done += 1
+
+        norm_sq = keep.tile([P, 1], F32)
+        nc.vector.tensor_reduce(out=norm_sq[:], in_=sum_sq[:, :pieces_done], axis=mybir.AxisListType.X, op=ALU.add)
+        clamped = keep.tile([P, 1], F32)
+        nc.vector.tensor_scalar_max(out=clamped[:], in0=norm_sq[:], scalar1=CLIP * CLIP)
+        factor = keep.tile([P, 1], F32)
+        nc.scalar.activation(
+            out=factor[:], in_=clamped[:], func=ACT.Abs_reciprocal_sqrt, scale=float(BATCH * BATCH) / (CLIP * CLIP)
+        )
+
+        for m in range(ALL_COLS // BANK):
+            cols = slice(BANK * m, BANK * (m + 1))
+            mean = psum_work.tile([P, BANK], F32, name="mean", tag="work")
+            nc.tensor.matmul(
+                out=mean[:], lhsT=factor[:, 0:1].to_broadcast([P, P]), rhs=resid[:, cols], start=True, stop=True
+            )
+            if m % 2 == 0:
+                nc.vector.tensor_copy(out=mean_row[0:1, cols], in_=mean[0:1, :])
+            else:
+                nc.scalar.copy(out=mean_row[0:1, cols], in_=mean[0:1, :])
+        nc.sync.dma_start(out=out.rearrange("(o n) -> o n", o=1), in_=mean_row[0:1, :])

@@ -117,9 +117,9 @@ def tile_gep_pb_k_kernel(
         for i in BASE_ORDER:
             for G in range(PASSES // OFFSETS):
                 for Q in range(4):
-                    nc.sync.dma_start(
-                        out=planes[i][32 * Q : 32 * Q + 16, G, :].bitcast(I32),
-                        in_=scales[i][OFFSETS * G : OFFSETS * (G + 1), 4 * Q : 4 * Q + 4, :].bitcast(I32),
+                    nc.gpsimd.dma_start(
+                        out=planes[i][32 * Q : 32 * Q + 16, G, :].bitcast(F32),
+                        in_=scales[i][OFFSETS * G : OFFSETS * (G + 1), 4 * Q : 4 * Q + 4, :].bitcast(F32),
                     )
 
         def regroup(unit):

@@ -30,7 +30,6 @@ X_LOAD = 8
 OFFSETS = 4
 W_BYTES = 9216
 W_BUFS = 10
-PIECE = 256
 
 FLOPS = 2 * BATCH * PASSES * K_PASS * ALL_COLS
 
@@ -156,7 +155,7 @@ def tile_gep_pb_k_kernel(
             waiting = (unit, grouped)
         quantise(waiting[0], waiting[1])
 
-        pieces_done = 0
+        groups_done = 0
         for i in BASE_ORDER:
             row_bytes = PACK * BASE_COLS[i]
             groups = cut_columns(BASE_COLS[i])
@@ -182,24 +181,29 @@ def tile_gep_pb_k_kernel(
                         )
                     g += 1
             for n, (start, width) in enumerate(groups):
-                for first in range(0, width, PIECE):
-                    size = min(PIECE, width - first)
-                    cols = slice(FIRST_COL[i] + start + first, FIRST_COL[i] + start + first + size)
-                    nc.vector.tensor_tensor(
-                        out=resid[:, cols], in0=grad[:, cols], in1=acc[n][:, first : first + size], op=ALU.subtract
-                    )
-                    nc.scalar.activation(
-                        out=squares[:, cols],
-                        in_=resid[:, cols],
-                        func=ACT.Square,
-                        accum_out=sum_sq[:, pieces_done : pieces_done + 1],
-                    )
-                    pieces_done += 1
+                cols = slice(FIRST_COL[i] + start, FIRST_COL[i] + start + width)
+                nc.vector.tensor_tensor(out=resid[:, cols], in0=grad[:, cols], in1=acc[n][:, :width], op=ALU.subtract)
+                nc.scalar.activation(
+                    out=squares[:, cols],
+                    in_=resid[:, cols],
+                    func=ACT.Square,
+                    accum_out=sum_sq[:, groups_done : groups_done + 1],
+                )
+                groups_done += 1
 
-        norm_sq = keep.tile([P, 1], F32)
-        nc.vector.tensor_reduce(out=norm_sq[:], in_=sum_sq[:, :pieces_done], axis=mybir.AxisListType.X, op=ALU.add)
+        earlier = keep.tile([P, 1], F32)
+        nc.vector.tensor_reduce(
+            out=earlier[:], in_=sum_sq[:, : groups_done - 1], axis=mybir.AxisListType.X, op=ALU.add
+        )
         clamped = keep.tile([P, 1], F32)
-        nc.vector.tensor_scalar_max(out=clamped[:], in0=norm_sq[:], scalar1=CLIP * CLIP)
+        nc.vector.tensor_scalar(
+            out=clamped[:],
+            in0=sum_sq[:, groups_done - 1 : groups_done],
+            scalar1=earlier[:, 0:1],
+            scalar2=CLIP * CLIP,
+            op0=ALU.add,
+            op1=ALU.max,
+        )
         factor = keep.tile([P, 1], F32)
         nc.scalar.activation(
             out=factor[:], in_=clamped[:], func=ACT.Abs_reciprocal_sqrt, scale=float(BATCH * BATCH) / (CLIP * CLIP)

@@ -30,6 +30,9 @@ X_LOAD = 8
 OFFSETS = 4
 W_BYTES = 9216
 W_BUFS = 10
+TERMS = 3
+BLOCKS = ALL_COLS // P
+MEAN_COLS = 4
 
 FLOPS = 2 * BATCH * PASSES * K_PASS * ALL_COLS
 
@@ -77,6 +80,7 @@ def tile_gep_pb_k_kernel(
         x_pool = ctx.enter_context(tc.tile_pool(name="x_pool", bufs=3 * PASSES // X_LOAD))
         stage = ctx.enter_context(tc.tile_pool(name="stage", bufs=3))
         w_pool = ctx.enter_context(tc.tile_pool(name="w_pool", bufs=W_BUFS))
+        scratch = ctx.enter_context(tc.tile_pool(name="scratch", bufs=3))
         psum_work = ctx.enter_context(tc.psum_pool(name="psum_work", bufs=5))
         psum_acc = ctx.enter_context(tc.psum_pool(name="psum_acc", bufs=1))
 
@@ -96,10 +100,14 @@ def tile_gep_pb_k_kernel(
         x_codes = keep.tile([P, 3 * PASSES, BATCH], U32, align_bytes=64)
         x_scales = keep.tile([P, 3 * PASSES, BATCH], U8, align_bytes=64)
         grad = keep.tile([P, ALL_COLS], BF16)
-        resid = keep.tile([P, ALL_COLS], F32)
-        squares = keep.tile([P, ALL_COLS], F32)
-        mean_row = keep.tile([P, ALL_COLS], F32)
-        sum_sq = keep.tile([P, ALL_COLS // P], F32)
+        r_terms = [keep.tile([P, ALL_COLS], BF16, name="r_term%d" % s) for s in range(TERMS)]
+        squares = keep.tile([P, BANK], F32)
+        sum_sq = keep.tile([P, BLOCKS], F32)
+        c_terms = keep.tile([P, MEAN_COLS], BF16)
+        nc.vector.memset(c_terms[:], 0.0)
+        mean_cols = keep.tile([P, P], F32)
+        nc.vector.memset(mean_cols[:], 0.0)
+        mean_rows = keep.tile([P, P], F32)
 
         x_words = {}
         for i in BASE_ORDER:
@@ -155,8 +163,7 @@ def tile_gep_pb_k_kernel(
             waiting = (unit, grouped)
         quantise(waiting[0], waiting[1])
 
-        groups_done = 0
-        for i in BASE_ORDER:
+        def product(i):
             row_bytes = PACK * BASE_COLS[i]
             groups = cut_columns(BASE_COLS[i])
             acc = [psum_acc.tile([P, BANK], F32, name="acc%d" % n) for n in range(len(groups))]
@@ -180,43 +187,87 @@ def tile_gep_pb_k_kernel(
                             stop=(g == PASSES - 1),
                         )
                     g += 1
-            for n, (start, width) in enumerate(groups):
-                cols = slice(FIRST_COL[i] + start, FIRST_COL[i] + start + width)
-                nc.vector.tensor_tensor(out=resid[:, cols], in0=grad[:, cols], in1=acc[n][:, :width], op=ALU.subtract)
+            return groups, acc
+
+        def residual(i, groups, acc, first_sum, cast):
+            spans = [(slice(FIRST_COL[i] + start, FIRST_COL[i] + start + width), width) for start, width in groups]
+            resid = []
+            for n, (cols, width) in enumerate(spans):
+                r = scratch.tile([P, BANK], F32, name="resid", tag="resid")
+                nc.vector.tensor_tensor(out=r[:, :width], in0=grad[:, cols], in1=acc[n][:, :width], op=ALU.subtract)
+                resid.append(r)
+            for n, (cols, width) in enumerate(spans):
                 nc.scalar.activation(
-                    out=squares[:, cols],
-                    in_=resid[:, cols],
+                    out=squares[:, :width],
+                    in_=resid[n][:, :width],
                     func=ACT.Square,
-                    accum_out=sum_sq[:, groups_done : groups_done + 1],
+                    accum_out=sum_sq[:, first_sum + n : first_sum + n + 1],
                 )
-                groups_done += 1
+                cast(out=r_terms[0][:, cols], in_=resid[n][:, :width])
+            rest = []
+            for n, (cols, width) in enumerate(spans):
+                d = scratch.tile([P, BANK], F32, name="rest", tag="rest")
+                nc.vector.tensor_tensor(
+                    out=d[:, :width], in0=resid[n][:, :width], in1=r_terms[0][:, cols], op=ALU.subtract
+                )
+                rest.append(d)
+            for n, (cols, width) in enumerate(spans):
+                cast(out=r_terms[1][:, cols], in_=rest[n][:, :width])
+            for n, (cols, width) in enumerate(spans):
+                nc.vector.tensor_tensor(
+                    out=r_terms[2][:, cols], in0=rest[n][:, :width], in1=r_terms[1][:, cols], op=ALU.subtract
+                )
+            return first_sum + len(spans)
+
+        sums_done = 0
+        for i in BASE_ORDER[:-1]:
+            groups, acc = product(i)
+            sums_done = residual(i, groups, acc, sums_done, nc.scalar.copy)
 
         earlier = keep.tile([P, 1], F32)
-        nc.vector.tensor_reduce(
-            out=earlier[:], in_=sum_sq[:, : groups_done - 1], axis=mybir.AxisListType.X, op=ALU.add
-        )
-        clamped = keep.tile([P, 1], F32)
-        nc.vector.tensor_scalar(
-            out=clamped[:],
-            in0=sum_sq[:, groups_done - 1 : groups_done],
-            scalar1=earlier[:, 0:1],
-            scalar2=CLIP * CLIP,
-            op0=ALU.add,
-            op1=ALU.max,
+        nc.vector.tensor_reduce(out=earlier[:], in_=sum_sq[:, :sums_done], axis=mybir.AxisListType.X, op=ALU.add)
+        earlier_less_clip = keep.tile([P, 1], F32)
+        nc.vector.tensor_scalar_add(out=earlier_less_clip[:], in0=earlier[:], scalar1=-CLIP * CLIP)
+
+        last = BASE_ORDER[-1]
+        groups, acc = product(last)
+        residual(last, groups, acc, sums_done, nc.vector.tensor_copy)
+
+        above = keep.tile([P, 1], F32)
+        nc.scalar.activation(
+            out=above[:], in_=sum_sq[:, sums_done : sums_done + 1], func=ACT.Relu, bias=earlier_less_clip[:, 0:1]
         )
         factor = keep.tile([P, 1], F32)
+        for dst in (factor[:], c_terms[:, 0:1]):
+            nc.scalar.activation(
+                out=dst,
+                in_=above[:],
+                func=ACT.Abs_reciprocal_sqrt,
+                scale=float(BATCH * BATCH) / (CLIP * CLIP),
+                bias=float(BATCH * BATCH),
+            )
+        c_rest = keep.tile([P, 1], F32)
+        for dst in (c_rest[:], c_terms[:, 1:2]):
+            nc.scalar.activation(out=dst, in_=c_terms[:, 0:1], func=ACT.Identity, scale=-1.0, bias=factor[:, 0:1])
         nc.scalar.activation(
-            out=factor[:], in_=clamped[:], func=ACT.Abs_reciprocal_sqrt, scale=float(BATCH * BATCH) / (CLIP * CLIP)
+            out=c_terms[:, 2:3], in_=c_terms[:, 1:2], func=ACT.Identity, scale=-1.0, bias=c_rest[:, 0:1]
         )
 
-        for m in range(ALL_COLS // BANK):
-            cols = slice(BANK * m, BANK * (m + 1))
-            mean = psum_work.tile([P, BANK], F32, name="mean", tag="work")
-            nc.tensor.matmul(
-                out=mean[:], lhsT=factor[:, 0:1].to_broadcast([P, P]), rhs=resid[:, cols], start=True, stop=True
-            )
-            if m % 2 == 0:
-                nc.vector.tensor_copy(out=mean_row[0:1, cols], in_=mean[0:1, :])
-            else:
-                nc.scalar.copy(out=mean_row[0:1, cols], in_=mean[0:1, :])
-        nc.sync.dma_start(out=out.rearrange("(o n) -> o n", o=1), in_=mean_row[0:1, :])
+        mean_ps = psum_work.tile([P, BLOCKS, MEAN_COLS], F32, name="mean_ps", tag="work")
+        blocks = [m for i in BASE_ORDER for m in range(FIRST_COL[i] // P, (FIRST_COL[i] + BASE_COLS[i]) // P)]
+        for m in blocks:
+            for s in range(TERMS):
+                nc.tensor.matmul(
+                    out=mean_ps[:, m, :],
+                    lhsT=r_terms[s][:, P * m : P * (m + 1)],
+                    rhs=c_terms[:],
+                    start=(s == 0),
+                    stop=(s == TERMS - 1),
+                )
+        nc.vector.tensor_reduce(out=mean_cols[:, :BLOCKS], in_=mean_ps[:], axis=mybir.AxisListType.X, op=ALU.add)
+        mean_t = psum_work.tile([P, P], F32, name="mean_t", tag="work")
+        nc.tensor.transpose(mean_t[:], mean_cols[:], ident[:])
+        nc.vector.tensor_copy(out=mean_rows[0:32, :], in_=mean_t[0:32, :])
+        out_rows = out.rearrange("(m j) -> m j", j=P)
+        nc.sync.dma_start(out=out_rows[0:16, :], in_=mean_rows[0:16, :])
+        nc.scalar.dma_start(out=out_rows[16:BLOCKS, :], in_=mean_rows[16:BLOCKS, :])

@@ -33,6 +33,7 @@ W_BUFS = 10
 TERMS = 3
 BLOCKS = ALL_COLS // P
 MEAN_COLS = 4
+IDLE_MATMULS = 4
 
 FLOPS = 2 * BATCH * PASSES * K_PASS * ALL_COLS
 
@@ -232,6 +233,10 @@ def tile_gep_pb_k_kernel(
         last = BASE_ORDER[-1]
         groups, acc = product(last)
         residual(last, groups, acc, sums_done, nc.vector.tensor_copy)
+
+        idle = psum_work.tile([P, BANK], F32, name="idle", tag="work")
+        for n in range(IDLE_MATMULS):
+            nc.tensor.matmul(out=idle[:], lhsT=grad[:, :P], rhs=grad[:, :BANK], start=True, stop=True)
 
         above = keep.tile([P, 1], F32)
         nc.scalar.activation(

@@ -33,6 +33,7 @@ W_BUFS = 10
 TERMS = 3
 BLOCKS = ALL_COLS // P
 MEAN_COLS = 4
+HELD_PASSES = 4
 IDLE_MATMULS = 4
 
 FLOPS = 2 * BATCH * PASSES * K_PASS * ALL_COLS
@@ -48,14 +49,12 @@ def cut_columns(total):
     return groups
 
 
-def cut_passes(per_load, taper):
-    sizes = [per_load] * (PASSES // per_load)
-    if taper:
-        last = sizes.pop()
-        while last > 1:
-            last //= 2
-            sizes.append(last)
-        sizes.append(last)
+def halve(passes):
+    sizes = []
+    while passes > 1:
+        passes //= 2
+        sizes.append(passes)
+    sizes.append(passes)
     return sizes
 
 
@@ -164,31 +163,32 @@ def tile_gep_pb_k_kernel(
             waiting = (unit, grouped)
         quantise(waiting[0], waiting[1])
 
-        def product(i):
-            row_bytes = PACK * BASE_COLS[i]
-            groups = cut_columns(BASE_COLS[i])
+        def product(i, groups, loads):
             acc = [psum_acc.tile([P, BANK], F32, name="acc%d" % n) for n in range(len(groups))]
-            g = 0
-            for n_passes in cut_passes(W_BYTES // row_bytes, taper=(i == BASE_ORDER[-1])):
+            for first_pass, n_passes, first_col, n_cols in loads:
+                row_bytes = PACK * n_cols
                 w = w_pool.tile([P, W_BYTES], U8, align_bytes=64)
                 nc.sync.dma_start(
                     out=w[:, : n_passes * row_bytes].bitcast(I32).rearrange("p (g c) -> p g c", g=n_passes),
-                    in_=words[i][g : g + n_passes].rearrange("g p n t -> p g (n t)").bitcast(I32),
+                    in_=words[i][first_pass : first_pass + n_passes, :, first_col : first_col + n_cols, :]
+                    .rearrange("g p n t -> p g (n t)")
+                    .bitcast(I32),
                 )
                 for local in range(n_passes):
+                    g = first_pass + local
                     for n, (start, width) in enumerate(groups):
-                        first_byte = local * row_bytes + PACK * start
-                        nc.tensor.matmul_mx(
-                            out=acc[n][:, :width],
-                            lhsT=x_codes[:, PASSES * i + g, :].bitcast(FP8X4),
-                            lhsT_scale=x_scales[:, PASSES * i + g, :],
-                            rhs=w[:, first_byte : first_byte + PACK * width].bitcast(FP8X4),
-                            rhs_scale=planes[i][4 * (g % OFFSETS) : P, g // OFFSETS, start : start + width],
-                            start=(g == 0),
-                            stop=(g == PASSES - 1),
-                        )
-                    g += 1
-            return groups, acc
+                        if first_col <= start and start + width <= first_col + n_cols:
+                            first_byte = local * row_bytes + PACK * (start - first_col)
+                            nc.tensor.matmul_mx(
+                                out=acc[n][:, :width],
+                                lhsT=x_codes[:, PASSES * i + g, :].bitcast(FP8X4),
+                                lhsT_scale=x_scales[:, PASSES * i + g, :],
+                                rhs=w[:, first_byte : first_byte + PACK * width].bitcast(FP8X4),
+                                rhs_scale=planes[i][4 * (g % OFFSETS) : P, g // OFFSETS, start : start + width],
+                                start=(g == 0),
+                                stop=(g == PASSES - 1),
+                            )
+            return acc
 
         def residual(i, groups, acc, first_sum, cast):
             spans = [(slice(FIRST_COL[i] + start, FIRST_COL[i] + start + width), width) for start, width in groups]
@@ -222,7 +222,9 @@ def tile_gep_pb_k_kernel(
 
         sums_done = 0
         for i in BASE_ORDER[:-1]:
-            groups, acc = product(i)
+            groups = cut_columns(BASE_COLS[i])
+            per_load = W_BYTES // (PACK * BASE_COLS[i])
+            acc = product(i, groups, [(g, per_load, 0, BASE_COLS[i]) for g in range(0, PASSES, per_load)])
             sums_done = residual(i, groups, acc, sums_done, nc.scalar.copy)
 
         earlier = keep.tile([P, 1], F32)
@@ -231,8 +233,70 @@ def tile_gep_pb_k_kernel(
         nc.vector.tensor_scalar_add(out=earlier_less_clip[:], in0=earlier[:], scalar1=-CLIP * CLIP)
 
         last = BASE_ORDER[-1]
-        groups, acc = product(last)
-        residual(last, groups, acc, sums_done, nc.vector.tensor_copy)
+        first = FIRST_COL[last]
+        late = BASE_COLS[last] - P
+        groups = cut_columns(late) + [(late, P)]
+        per_load = W_BYTES // (PACK * BASE_COLS[last])
+        held = PASSES - HELD_PASSES
+        loads = [(g, per_load, 0, BASE_COLS[last]) for g in range(0, held, per_load)]
+        loads.append((held, HELD_PASSES, 0, late))
+        g = held
+        for n_passes in halve(HELD_PASSES):
+            loads.append((g, n_passes, late, P))
+            g += n_passes
+        acc = product(last, groups, loads)
+
+        r = scratch.tile([P, BANK], F32, name="resid", tag="resid")
+        d = scratch.tile([P, BANK], F32, name="rest", tag="rest")
+
+        def subtract(n):
+            start, width = groups[n]
+            nc.vector.tensor_tensor(
+                out=r[:, start : start + width],
+                in0=grad[:, first + start : first + start + width],
+                in1=acc[n][:, :width],
+                op=ALU.subtract,
+            )
+
+        def square(lo, hi, k):
+            nc.scalar.activation(
+                out=squares[:, lo:hi], in_=r[:, lo:hi], func=ACT.Square, accum_out=sum_sq[:, k : k + 1]
+            )
+
+        def cut(step, lo, hi):
+            cols = slice(first + lo, first + hi)
+            if step == 0:
+                nc.vector.tensor_copy(out=r_terms[0][:, cols], in_=r[:, lo:hi])
+            elif step == 1:
+                nc.vector.tensor_tensor(out=d[:, lo:hi], in0=r[:, lo:hi], in1=r_terms[0][:, cols], op=ALU.subtract)
+            elif step == 2:
+                nc.vector.tensor_copy(out=r_terms[1][:, cols], in_=d[:, lo:hi])
+            else:
+                nc.vector.tensor_tensor(
+                    out=r_terms[2][:, cols], in0=d[:, lo:hi], in1=r_terms[1][:, cols], op=ALU.subtract
+                )
+
+        for n in range(len(groups) - 1):
+            subtract(n)
+        square(0, late, sums_done)
+        all_but_late = keep.tile([P, 1], F32)
+        nc.scalar.activation(
+            out=all_but_late[:],
+            in_=sum_sq[:, sums_done : sums_done + 1],
+            func=ACT.Identity,
+            bias=earlier_less_clip[:, 0:1],
+        )
+        sums_done += 1
+        cut(0, 0, late)
+        subtract(len(groups) - 1)
+        square(late, late + P, sums_done)
+        cut(1, 0, late)
+        cut(0, late, late + P)
+        cut(2, 0, late)
+        cut(1, late, late + P)
+        cut(3, 0, late)
+        cut(2, late, late + P)
+        cut(3, late, late + P)
 
         idle = psum_work.tile([P, BANK], F32, name="idle", tag="work")
         for n in range(IDLE_MATMULS):
@@ -240,7 +304,7 @@ def tile_gep_pb_k_kernel(
 
         above = keep.tile([P, 1], F32)
         nc.scalar.activation(
-            out=above[:], in_=sum_sq[:, sums_done : sums_done + 1], func=ACT.Relu, bias=earlier_less_clip[:, 0:1]
+            out=above[:], in_=sum_sq[:, sums_done : sums_done + 1], func=ACT.Relu, bias=all_but_late[:, 0:1]
         )
         factor = keep.tile([P, 1], F32)
         for dst in (factor[:], c_terms[:, 0:1]):

@@ -99,7 +99,7 @@ def tile_gep_pb_k_kernel(
 
         x_codes = keep.tile([P, 3 * PASSES, BATCH], U32, align_bytes=64)
         x_scales = keep.tile([P, 3 * PASSES, BATCH], U8, align_bytes=64)
-        grad = keep.tile([P, ALL_COLS], BF16)
+        grad = keep.tile([P, ALL_COLS], BF16, align_bytes=256)
         r_terms = [keep.tile([P, ALL_COLS], BF16, name="r_term%d" % s) for s in range(TERMS)]
         squares = keep.tile([P, BANK], F32)
         sum_sq = keep.tile([P, BLOCKS], F32)
@@ -113,7 +113,7 @@ def tile_gep_pb_k_kernel(
         for i in BASE_ORDER:
             for load in range(PASSES // X_LOAD):
                 first_pass = PASSES * i + X_LOAD * load
-                x_sb = x_pool.tile([P, X_LOAD * K_PASS], BF16)
+                x_sb = x_pool.tile([P, X_LOAD * K_PASS], BF16, align_bytes=256)
                 nc.sync.dma_start(
                     out=x_sb[:],
                     in_=embedding[:, K_PASS * first_pass : K_PASS * (first_pass + X_LOAD)],
@@ -167,7 +167,7 @@ def tile_gep_pb_k_kernel(
             acc = [psum_acc.tile([P, BANK], F32, name="acc%d" % n) for n in range(len(groups))]
             for first_pass, n_passes, first_col, n_cols in loads:
                 row_bytes = PACK * n_cols
-                w = w_pool.tile([P, W_BYTES], U8, align_bytes=64)
+                w = w_pool.tile([P, W_BYTES], U8, align_bytes=256)
                 nc.sync.dma_start(
                     out=w[:, : n_passes * row_bytes].bitcast(I32).rearrange("p (g c) -> p g c", g=n_passes),
                     in_=words[i][first_pass : first_pass + n_passes, :, first_col : first_col + n_cols, :]

@@ -86,9 +86,8 @@ def tile_gep_pb_k_kernel(
 
         planes = {}
         for i in BASE_ORDER:
-            planes[i] = keep.tile(
-                [P, PASSES // OFFSETS, BASE_COLS[i]], U8, name="planes%d" % i, align_bytes=64
-            )
+            pitch = -(-BASE_COLS[i] // 256) * 256
+            planes[i] = keep.tile([P, PASSES // OFFSETS, pitch], U8, name="planes%d" % i, align_bytes=256)
             nc.vector.memset(planes[i][:].bitcast(I32), 0)
         one = keep.tile([P, 1], F32)
         nc.vector.memset(one[:], 1.0)
@@ -107,7 +106,7 @@ def tile_gep_pb_k_kernel(
         nc.vector.memset(c_terms[:], 0.0)
         mean_cols = keep.tile([P, P], F32)
         nc.vector.memset(mean_cols[:], 0.0)
-        mean_rows = keep.tile([P, P], F32)
+        mean_rows = keep.tile([P, P], F32, align_bytes=256)
 
         x_words = {}
         for i in BASE_ORDER:
@@ -125,7 +124,7 @@ def tile_gep_pb_k_kernel(
             for G in range(PASSES // OFFSETS):
                 for Q in range(4):
                     nc.gpsimd.dma_start(
-                        out=planes[i][32 * Q : 32 * Q + 16, G, :].bitcast(F32),
+                        out=planes[i][32 * Q : 32 * Q + 16, G, : BASE_COLS[i]].bitcast(F32),
                         in_=scales[i][OFFSETS * G : OFFSETS * (G + 1), 4 * Q : 4 * Q + 4, :].bitcast(F32),
                     )
 

@@ -98,7 +98,7 @@ def tile_gep_pb_k_kernel(
 
         x_codes = keep.tile([P, 3 * PASSES, BATCH], U32, align_bytes=64)
         x_scales = keep.tile([P, 3 * PASSES, BATCH], U8, align_bytes=64)
-        grad = keep.tile([P, ALL_COLS], BF16, align_bytes=256)
+        grad = keep.tile([P, ALL_COLS], BF16, align_bytes=1024)
         r_terms = [keep.tile([P, ALL_COLS], BF16, name="r_term%d" % s) for s in range(TERMS)]
         squares = keep.tile([P, BANK], F32)
         sum_sq = keep.tile([P, BLOCKS], F32)
@@ -112,7 +112,7 @@ def tile_gep_pb_k_kernel(
         for i in BASE_ORDER:
             for load in range(PASSES // X_LOAD):
                 first_pass = PASSES * i + X_LOAD * load
-                x_sb = x_pool.tile([P, X_LOAD * K_PASS], BF16, align_bytes=256)
+                x_sb = x_pool.tile([P, X_LOAD * K_PASS], BF16, align_bytes=1024)
                 nc.sync.dma_start(
                     out=x_sb[:],
                     in_=embedding[:, K_PASS * first_pass : K_PASS * (first_pass + X_LOAD)],
@@ -166,7 +166,7 @@ def tile_gep_pb_k_kernel(
             acc = [psum_acc.tile([P, BANK], F32, name="acc%d" % n) for n in range(len(groups))]
             for first_pass, n_passes, first_col, n_cols in loads:
                 row_bytes = PACK * n_cols
-                w = w_pool.tile([P, W_BYTES], U8, align_bytes=256)
+                w = w_pool.tile([P, W_BYTES], U8, align_bytes=1024)
                 nc.sync.dma_start(
                     out=w[:, : n_passes * row_bytes].bitcast(I32).rearrange("p (g c) -> p g c", g=n_passes),
                     in_=words[i][first_pass : first_pass + n_passes, :, first_col : first_col + n_cols, :]

@@ -34,7 +34,7 @@ TERMS = 3
 BLOCKS = ALL_COLS // P
 MEAN_COLS = 4
 HELD_PASSES = 4
-IDLE_MATMULS = 4
+IDLE_MATMULS = 6
 
 FLOPS = 2 * BATCH * PASSES * K_PASS * ALL_COLS
 

from contextlib import ExitStack

import concourse.mybir as mybir
from concourse.masks import make_identity

F32 = mybir.dt.float32
BF16 = mybir.dt.bfloat16
I32 = mybir.dt.int32
U32 = mybir.dt.uint32
U8 = mybir.dt.uint8
FP8X4 = mybir.dt.float8_e4m3fn_x4
ACT = mybir.ActivationFunctionType
ALU = mybir.AluOpType

P = 128
BATCH = 128
PACK = 4
K_PASS = P * PACK
PASSES = 16
BASE_COLS = (512, 1152, 896)
FIRST_COL = (0, 512, 1664)
ALL_COLS = 2560
CLIP = 1.0
BANK = 512

BASE_ORDER = (1, 2, 0)

UNIT = 4
X_LOAD = 8
OFFSETS = 4
W_BYTES = 9216
W_BUFS = 10
TERMS = 3
BLOCKS = ALL_COLS // P
MEAN_COLS = 4
HELD_PASSES = 4
IDLE_MATMULS = 6

FLOPS = 2 * BATCH * PASSES * K_PASS * ALL_COLS


def cut_columns(total):
    groups = []
    start = 0
    for width in (512, 256, 128):
        while total - start >= width:
            groups.append((start, width))
            start += width
    return groups


def halve(passes):
    sizes = []
    while passes > 1:
        passes //= 2
        sizes.append(passes)
    sizes.append(passes)
    return sizes


def tile_gep_pb_k_kernel(
    tc,
    target_grad,
    embedding,
    bases0_words,
    bases0_scales,
    bases1_words,
    bases1_scales,
    bases2_words,
    bases2_scales,
    out,
):
    nc = tc.nc
    words = (bases0_words, bases1_words, bases2_words)
    scales = (bases0_scales, bases1_scales, bases2_scales)

    with ExitStack() as ctx:
        ctx.enter_context(tc.manual_schedule())
        keep = ctx.enter_context(tc.tile_pool(name="keep", bufs=1))
        x_pool = ctx.enter_context(tc.tile_pool(name="x_pool", bufs=3 * PASSES // X_LOAD))
        stage = ctx.enter_context(tc.tile_pool(name="stage", bufs=3))
        w_pool = ctx.enter_context(tc.tile_pool(name="w_pool", bufs=W_BUFS))
        scratch = ctx.enter_context(tc.tile_pool(name="scratch", bufs=3))
        psum_work = ctx.enter_context(tc.psum_pool(name="psum_work", bufs=5))
        psum_acc = ctx.enter_context(tc.psum_pool(name="psum_acc", bufs=1))

        planes = {}
        for i in BASE_ORDER:
            pitch = -(-BASE_COLS[i] // 256) * 256
            planes[i] = keep.tile([P, PASSES // OFFSETS, pitch], U8, name="planes%d" % i, align_bytes=256)
            nc.vector.memset(planes[i][:].bitcast(I32), 0)
        one = keep.tile([P, 1], F32)
        nc.vector.memset(one[:], 1.0)
        warm = keep.tile([P, 1], F32)
        nc.scalar.activation(out=warm[:], in_=one[:], func=ACT.Abs_reciprocal_sqrt)
        ident = keep.tile([P, P], F32)
        make_identity(nc, ident[:])

        x_codes = keep.tile([P, 3 * PASSES, BATCH], U32, align_bytes=64)
        x_scales = keep.tile([P, 3 * PASSES, BATCH], U8, align_bytes=64)
        grad = keep.tile([P, ALL_COLS], BF16, align_bytes=1024)
        r_terms = [keep.tile([P, ALL_COLS], BF16, name="r_term%d" % s) for s in range(TERMS)]
        squares = keep.tile([P, BANK], F32)
        sum_sq = keep.tile([P, BLOCKS], F32)
        c_terms = keep.tile([P, MEAN_COLS], BF16)
        nc.vector.memset(c_terms[:], 0.0)
        mean_cols = keep.tile([P, P], F32)
        nc.vector.memset(mean_cols[:], 0.0)
        mean_rows = keep.tile([P, P], F32, align_bytes=256)

        x_words = {}
        for i in BASE_ORDER:
            for load in range(PASSES // X_LOAD):
                first_pass = PASSES * i + X_LOAD * load
                x_sb = x_pool.tile([P, X_LOAD * K_PASS], BF16, align_bytes=1024)
                nc.sync.dma_start(
                    out=x_sb[:],
                    in_=embedding[:, K_PASS * first_pass : K_PASS * (first_pass + X_LOAD)],
                )
                for g in range(X_LOAD):
                    x_words[first_pass + g] = x_sb[:, K_PASS * g : K_PASS * (g + 1)].bitcast(F32)
        nc.sync.dma_start(out=grad[:], in_=target_grad)
        for i in BASE_ORDER:
            for G in range(PASSES // OFFSETS):
                for Q in range(4):
                    nc.gpsimd.dma_start(
                        out=planes[i][32 * Q : 32 * Q + 16, G, : BASE_COLS[i]].bitcast(F32),
                        in_=scales[i][OFFSETS * G : OFFSETS * (G + 1), 4 * Q : 4 * Q + 4, :].bitcast(F32),
                    )

        def regroup(unit):
            grouped = stage.tile([P, UNIT, BATCH, PACK], BF16, align_bytes=64)
            grouped_words = grouped[:].bitcast(F32)
            for half in range(2):
                xt = psum_work.tile([P, UNIT // 2, 2, BATCH], F32, name="xt", tag="work")
                for j in range(UNIT // 2):
                    x_pass = UNIT * unit + (UNIT // 2) * half + j
                    for u in range(2):
                        nc.tensor.transpose(xt[:, j, u, :], x_words[x_pass][:, u : K_PASS // 2 : 2], ident[:])
                dst = grouped_words[:, (UNIT // 2) * half : (UNIT // 2) * (half + 1), :, :]
                src = xt[:].rearrange("p j u b -> p j b u")
                if half == 0:
                    nc.scalar.copy(out=dst, in_=src)
                else:
                    nc.vector.tensor_copy(out=dst, in_=src)
            return grouped

        def quantise(unit, grouped):
            passes = slice(UNIT * unit, UNIT * (unit + 1))
            nc.vector.quantize_mx(
                out=x_codes[:, passes, :].rearrange("p g b -> p (g b)").bitcast(FP8X4),
                scales=x_scales[:, passes, :].rearrange("p g b -> p (g b)"),
                in_=grouped[:].rearrange("p g b t -> p (g b t)"),
            )

        units = [PASSES // UNIT * i + n for i in BASE_ORDER for n in range(PASSES // UNIT)]
        waiting = None
        for unit in units:
            grouped = regroup(unit)
            if waiting is not None:
                quantise(waiting[0], waiting[1])
            waiting = (unit, grouped)
        quantise(waiting[0], waiting[1])

        def product(i, groups, loads):
            acc = [psum_acc.tile([P, BANK], F32, name="acc%d" % n) for n in range(len(groups))]
            for first_pass, n_passes, first_col, n_cols in loads:
                row_bytes = PACK * n_cols
                w = w_pool.tile([P, W_BYTES], U8, align_bytes=1024)
                nc.sync.dma_start(
                    out=w[:, : n_passes * row_bytes].bitcast(I32).rearrange("p (g c) -> p g c", g=n_passes),
                    in_=words[i][first_pass : first_pass + n_passes, :, first_col : first_col + n_cols, :]
                    .rearrange("g p n t -> p g (n t)")
                    .bitcast(I32),
                )
                for local in range(n_passes):
                    g = first_pass + local
                    for n, (start, width) in enumerate(groups):
                        if first_col <= start and start + width <= first_col + n_cols:
                            first_byte = local * row_bytes + PACK * (start - first_col)
                            nc.tensor.matmul_mx(
                                out=acc[n][:, :width],
                                lhsT=x_codes[:, PASSES * i + g, :].bitcast(FP8X4),
                                lhsT_scale=x_scales[:, PASSES * i + g, :],
                                rhs=w[:, first_byte : first_byte + PACK * width].bitcast(FP8X4),
                                rhs_scale=planes[i][4 * (g % OFFSETS) : P, g // OFFSETS, start : start + width],
                                start=(g == 0),
                                stop=(g == PASSES - 1),
                            )
            return acc

        def residual(i, groups, acc, first_sum, cast):
            spans = [(slice(FIRST_COL[i] + start, FIRST_COL[i] + start + width), width) for start, width in groups]
            resid = []
            for n, (cols, width) in enumerate(spans):
                r = scratch.tile([P, BANK], F32, name="resid", tag="resid")
                nc.vector.tensor_tensor(out=r[:, :width], in0=grad[:, cols], in1=acc[n][:, :width], op=ALU.subtract)
                resid.append(r)
            for n, (cols, width) in enumerate(spans):
                nc.scalar.activation(
                    out=squares[:, :width],
                    in_=resid[n][:, :width],
                    func=ACT.Square,
                    accum_out=sum_sq[:, first_sum + n : first_sum + n + 1],
                )
                cast(out=r_terms[0][:, cols], in_=resid[n][:, :width])
            rest = []
            for n, (cols, width) in enumerate(spans):
                d = scratch.tile([P, BANK], F32, name="rest", tag="rest")
                nc.vector.tensor_tensor(
                    out=d[:, :width], in0=resid[n][:, :width], in1=r_terms[0][:, cols], op=ALU.subtract
                )
                rest.append(d)
            for n, (cols, width) in enumerate(spans):
                cast(out=r_terms[1][:, cols], in_=rest[n][:, :width])
            for n, (cols, width) in enumerate(spans):
                nc.vector.tensor_tensor(
                    out=r_terms[2][:, cols], in0=rest[n][:, :width], in1=r_terms[1][:, cols], op=ALU.subtract
                )
            return first_sum + len(spans)

        sums_done = 0
        for i in BASE_ORDER[:-1]:
            groups = cut_columns(BASE_COLS[i])
            per_load = W_BYTES // (PACK * BASE_COLS[i])
            acc = product(i, groups, [(g, per_load, 0, BASE_COLS[i]) for g in range(0, PASSES, per_load)])
            sums_done = residual(i, groups, acc, sums_done, nc.scalar.copy)

        earlier = keep.tile([P, 1], F32)
        nc.vector.tensor_reduce(out=earlier[:], in_=sum_sq[:, :sums_done], axis=mybir.AxisListType.X, op=ALU.add)
        earlier_less_clip = keep.tile([P, 1], F32)
        nc.vector.tensor_scalar_add(out=earlier_less_clip[:], in0=earlier[:], scalar1=-CLIP * CLIP)

        last = BASE_ORDER[-1]
        first = FIRST_COL[last]
        late = BASE_COLS[last] - P
        groups = cut_columns(late) + [(late, P)]
        per_load = W_BYTES // (PACK * BASE_COLS[last])
        held = PASSES - HELD_PASSES
        loads = [(g, per_load, 0, BASE_COLS[last]) for g in range(0, held, per_load)]
        loads.append((held, HELD_PASSES, 0, late))
        g = held
        for n_passes in halve(HELD_PASSES):
            loads.append((g, n_passes, late, P))
            g += n_passes
        acc = product(last, groups, loads)

        r = scratch.tile([P, BANK], F32, name="resid", tag="resid")
        d = scratch.tile([P, BANK], F32, name="rest", tag="rest")

        def subtract(n):
            start, width = groups[n]
            nc.vector.tensor_tensor(
                out=r[:, start : start + width],
                in0=grad[:, first + start : first + start + width],
                in1=acc[n][:, :width],
                op=ALU.subtract,
            )

        def square(lo, hi, k):
            nc.scalar.activation(
                out=squares[:, lo:hi], in_=r[:, lo:hi], func=ACT.Square, accum_out=sum_sq[:, k : k + 1]
            )

        def cut(step, lo, hi):
            cols = slice(first + lo, first + hi)
            if step == 0:
                nc.vector.tensor_copy(out=r_terms[0][:, cols], in_=r[:, lo:hi])
            elif step == 1:
                nc.vector.tensor_tensor(out=d[:, lo:hi], in0=r[:, lo:hi], in1=r_terms[0][:, cols], op=ALU.subtract)
            elif step == 2:
                nc.vector.tensor_copy(out=r_terms[1][:, cols], in_=d[:, lo:hi])
            else:
                nc.vector.tensor_tensor(
                    out=r_terms[2][:, cols], in0=d[:, lo:hi], in1=r_terms[1][:, cols], op=ALU.subtract
                )

        for n in range(len(groups) - 1):
            subtract(n)
        square(0, late, sums_done)
        all_but_late = keep.tile([P, 1], F32)
        nc.scalar.activation(
            out=all_but_late[:],
            in_=sum_sq[:, sums_done : sums_done + 1],
            func=ACT.Identity,
            bias=earlier_less_clip[:, 0:1],
        )
        sums_done += 1
        cut(0, 0, late)
        subtract(len(groups) - 1)
        square(late, late + P, sums_done)
        cut(1, 0, late)
        cut(0, late, late + P)
        cut(2, 0, late)
        cut(1, late, late + P)
        cut(3, 0, late)
        cut(2, late, late + P)
        cut(3, late, late + P)

        idle = psum_work.tile([P, BANK], F32, name="idle", tag="work")
        for n in range(IDLE_MATMULS):
            nc.tensor.matmul(out=idle[:], lhsT=grad[:, :P], rhs=grad[:, :BANK], start=True, stop=True)

        above = keep.tile([P, 1], F32)
        nc.scalar.activation(
            out=above[:], in_=sum_sq[:, sums_done : sums_done + 1], func=ACT.Relu, bias=all_but_late[:, 0:1]
        )
        factor = keep.tile([P, 1], F32)
        for dst in (factor[:], c_terms[:, 0:1]):
            nc.scalar.activation(
                out=dst,
                in_=above[:],
                func=ACT.Abs_reciprocal_sqrt,
                scale=float(BATCH * BATCH) / (CLIP * CLIP),
                bias=float(BATCH * BATCH),
            )
        c_rest = keep.tile([P, 1], F32)
        for dst in (c_rest[:], c_terms[:, 1:2]):
            nc.scalar.activation(out=dst, in_=c_terms[:, 0:1], func=ACT.Identity, scale=-1.0, bias=factor[:, 0:1])
        nc.scalar.activation(
            out=c_terms[:, 2:3], in_=c_terms[:, 1:2], func=ACT.Identity, scale=-1.0, bias=c_rest[:, 0:1]
        )

        mean_ps = psum_work.tile([P, BLOCKS, MEAN_COLS], F32, name="mean_ps", tag="work")
        blocks = [m for i in BASE_ORDER for m in range(FIRST_COL[i] // P, (FIRST_COL[i] + BASE_COLS[i]) // P)]
        for m in blocks:
            for s in range(TERMS):
                nc.tensor.matmul(
                    out=mean_ps[:, m, :],
                    lhsT=r_terms[s][:, P * m : P * (m + 1)],
                    rhs=c_terms[:],
                    start=(s == 0),
                    stop=(s == TERMS - 1),
                )
        nc.vector.tensor_reduce(out=mean_cols[:, :BLOCKS], in_=mean_ps[:], axis=mybir.AxisListType.X, op=ALU.add)
        mean_t = psum_work.tile([P, P], F32, name="mean_t", tag="work")
        nc.tensor.transpose(mean_t[:], mean_cols[:], ident[:])
        nc.vector.tensor_copy(out=mean_rows[0:32, :], in_=mean_t[0:32, :])
        out_rows = out.rearrange("(m j) -> m j", j=P)
        nc.sync.dma_start(out=out_rows[0:16, :], in_=mean_rows[0:16, :])
        nc.scalar.dma_start(out=out_rows[16:BLOCKS, :], in_=mean_rows[16:BLOCKS, :])
